import numpy as np
import ml_dtypes

BF16 = ml_dtypes.bfloat16


def bf(x):
    return np.asarray(x, np.float32).astype(BF16)


def f32(x):
    return np.asarray(x, np.float32)


def f64(x):
    return np.asarray(x).astype(np.float64)


def striped(idx):
    return np.tile(idx.reshape(-1, 16).T, (8, 1))


B, HEADS, L, C, S, D, N, NB = 4, 2, 512, 1024, 256, 256, 512, 128


def setup_inputs():
    return {"x": f32(0.2 * np.exp(np.random.standard_normal((B, C, S)))), "t_att": f32(0.2 * np.exp(np.random.standard_normal((C, N)))), "context": bf(2.0 * np.random.standard_normal((B, L, D))), "offs": striped(np.concatenate([np.random.permutation(S)[:NB] for _ in range(B)]))}


def reference(x, t_att, context, offs):
    idx = offs[:16].T.reshape(-1)
    res = np.zeros((D, N), np.float64)
    for b in range(B):
        lo, hi = b * NB, (b + 1) * NB
        prod = f64(x)[b][:, idx[lo:hi]] * f64(t_att)[:, lo:hi]
        a = prod.reshape(HEADS, L, NB).sum(axis=0)
        z = a.sum(axis=0, keepdims=True)
        res[:, lo:hi] = (f64(context)[b].T @ a) / z
    return res

@@ -1,0 +1,89 @@
+import concourse.mybir as mybir
+
+F32 = mybir.dt.float32
+BF16 = mybir.dt.bfloat16
+U16 = mybir.dt.uint16
+MULT = mybir.AluOpType.mult
+ADD = mybir.AluOpType.add
+
+P = 128
+DOCS = 4
+HEADS = 2
+TOKENS = 512
+ENTITIES = 256
+FEATURES = 256
+PAIRS = 128
+ENTRIES = DOCS * PAIRS
+TOKEN_BLOCKS = TOKENS // P
+FEATURE_BLOCKS = FEATURES // P
+
+FLOPS = 2 * TOKENS * (FEATURES + 1) * ENTRIES
+
+
+def tile_my_model4_kernel(tc, x, t_att, context, offs, out):
+    nc = tc.nc
+
+    x_rows = x.rearrange("b (q p t) e -> b q t p e", q=HEADS, t=TOKEN_BLOCKS)
+    t_att_rows = t_att.rearrange("(q p t) j -> q p t j", q=HEADS, t=TOKEN_BLOCKS)
+    context_rows = context.rearrange("b (p t) d -> b p t d", t=TOKEN_BLOCKS)
+    out_rows = out.rearrange("(c p) j -> p c j", p=P)
+
+    with (
+        tc.tile_pool(name="held", bufs=1) as held,
+        tc.tile_pool(name="work", bufs=2) as work,
+        tc.psum_pool(name="psum", bufs=2) as psum,
+    ):
+        offsets = held.tile([P, ENTRIES // 16], U16, name="offsets")
+        nc.sync.dma_start(offsets[:], offs)
+
+        ones = held.tile([P, P], BF16, name="ones")
+        nc.vector.memset(ones[:], 1.0)
+
+        windows = {}
+        tails = {}
+        features = {}
+        for b in range(DOCS):
+            pairs = slice(b * PAIRS, (b + 1) * PAIRS)
+            tails[b] = held.tile([P, HEADS, TOKEN_BLOCKS, PAIRS], F32, name=f"tail{b}")
+            for q in range(HEADS):
+                nc.scalar.dma_start(tails[b][:, q], t_att_rows[q, :, :, pairs])
+            for t in range(TOKEN_BLOCKS):
+                for q in range(HEADS):
+                    windows[b, q, t] = held.tile([P, ENTITIES], F32, name=f"window{b}{q}{t}")
+                    nc.sync.dma_start(windows[b, q, t][:], x_rows[b, q, t])
+            features[b] = held.tile([P, TOKEN_BLOCKS, FEATURES], BF16, name=f"features{b}")
+            nc.scalar.dma_start(features[b][:], context_rows[b])
+
+        for b in range(DOCS):
+            pairs = slice(b * PAIRS, (b + 1) * PAIRS)
+            picks = offsets[:, b * (PAIRS // 16) : (b + 1) * (PAIRS // 16)]
+
+            products = work.tile([P, HEADS, TOKEN_BLOCKS, PAIRS], F32, name="products")
+            for t in range(TOKEN_BLOCKS):
+                for q in range(HEADS):
+                    nc.vector.tensor_tensor(
+                        products[:, q, t], windows[b, q, t][:].indirect(picks), tails[b][:, q, t], MULT
+                    )
+
+            weights = work.tile([P, TOKEN_BLOCKS, PAIRS], BF16, name="weights")
+            nc.vector.tensor_tensor(weights[:], products[:, 0], products[:, 1], ADD)
+
+            z_all = psum.tile([P, PAIRS], F32, name="z_all")
+            for t in range(TOKEN_BLOCKS):
+                nc.tensor.matmul(
+                    z_all[:], ones[:], weights[:, t], start=(t == 0), stop=(t == TOKEN_BLOCKS - 1)
+                )
+            z_inverse = work.tile([P, PAIRS], F32, name="z_inverse")
+            nc.vector.reciprocal(z_inverse[:], z_all[:])
+
+            pooled = work.tile([P, FEATURE_BLOCKS, PAIRS], F32, name="pooled")
+            for c in range(FEATURE_BLOCKS):
+                block = slice(c * P, (c + 1) * P)
+                sums = psum.tile([P, PAIRS], F32, name="sums")
+                for t in range(TOKEN_BLOCKS):
+                    nc.tensor.matmul(
+                        sums[:], features[b][:, t, block], weights[:, t],
+                        start=(t == 0), stop=(t == TOKEN_BLOCKS - 1),
+                    )
+                nc.vector.tensor_tensor(pooled[:, c], sums[:], z_inverse[:], MULT)
+            nc.sync.dma_start(out_rows[:, :, pairs], pooled[:])

@@ -1,10 +1,12 @@
 import concourse.mybir as mybir
+from concourse.masks import make_identity
 
 F32 = mybir.dt.float32
 BF16 = mybir.dt.bfloat16
 U16 = mybir.dt.uint16
 MULT = mybir.AluOpType.mult
 ADD = mybir.AluOpType.add
+COPY = mybir.ActivationFunctionType.Copy
 
 P = 128
 DOCS = 4
@@ -30,60 +32,65 @@ def tile_my_model4_kernel(tc, x, t_att, context, offs, out):
 
     with (
         tc.tile_pool(name="held", bufs=1) as held,
-        tc.tile_pool(name="work", bufs=2) as work,
+        tc.tile_pool(name="work", bufs=4) as work,
         tc.psum_pool(name="psum", bufs=2) as psum,
     ):
         offsets = held.tile([P, ENTRIES // 16], U16, name="offsets")
         nc.sync.dma_start(offsets[:], offs)
 
-        ones = held.tile([P, P], BF16, name="ones")
+        ones = held.tile([P, 1], BF16, name="ones")
         nc.vector.memset(ones[:], 1.0)
+        identity = held.tile([P, P], F32, name="identity")
+        make_identity(nc, identity[:])
 
+        queue = (nc.sync, nc.scalar)
         windows = {}
         tails = {}
         features = {}
         for b in range(DOCS):
-            pairs = slice(b * PAIRS, (b + 1) * PAIRS)
-            tails[b] = held.tile([P, HEADS, TOKEN_BLOCKS, PAIRS], F32, name=f"tail{b}")
-            for q in range(HEADS):
-                nc.scalar.dma_start(tails[b][:, q], t_att_rows[q, :, :, pairs])
+            if b % 2 == 0:
+                columns = slice(b * PAIRS, (b + 2) * PAIRS)
+                for q in range(HEADS):
+                    tails[b // 2, q] = held.tile([P, TOKEN_BLOCKS, 2 * PAIRS], F32, name=f"tail{b // 2}{q}")
+                    queue[q].dma_start(tails[b // 2, q][:], t_att_rows[q, :, :, columns])
             for t in range(TOKEN_BLOCKS):
                 for q in range(HEADS):
                     windows[b, q, t] = held.tile([P, ENTITIES], F32, name=f"window{b}{q}{t}")
-                    nc.sync.dma_start(windows[b, q, t][:], x_rows[b, q, t])
+                    queue[q].dma_start(windows[b, q, t][:], x_rows[b, q, t])
             features[b] = held.tile([P, TOKEN_BLOCKS, FEATURES], BF16, name=f"features{b}")
-            nc.scalar.dma_start(features[b][:], context_rows[b])
+            queue[b % 2].dma_start(features[b][:], context_rows[b])
+
+        sums = {}
+        z = {}
+
+        def normalise_and_store(b):
+            z_inverse = work.tile([P, 1], F32, name="z_inverse")
+            nc.vector.reciprocal(z_inverse[:], z[b][:])
+            pooled = work.tile([P, FEATURES], F32, name="pooled")
+            nc.scalar.activation(pooled[:], sums[b][:], COPY, scale=z_inverse[:])
+            flipped = psum.tile([P, FEATURE_BLOCKS, PAIRS], F32, name="flipped")
+            for c in range(FEATURE_BLOCKS):
+                nc.tensor.transpose(flipped[:, c], pooled[:, c * P : (c + 1) * P], identity[:])
+            result = work.tile([P, FEATURE_BLOCKS, PAIRS], F32, name="result")
+            nc.scalar.copy(result[:], flipped[:])
+            nc.sync.dma_start(out_rows[:, :, b * PAIRS : (b + 1) * PAIRS], result[:])
 
         for b in range(DOCS):
-            pairs = slice(b * PAIRS, (b + 1) * PAIRS)
             picks = offsets[:, b * (PAIRS // 16) : (b + 1) * (PAIRS // 16)]
-
-            products = work.tile([P, HEADS, TOKEN_BLOCKS, PAIRS], F32, name="products")
+            columns = slice((b % 2) * PAIRS, (b % 2 + 1) * PAIRS)
+            sums[b] = psum.tile([P, FEATURES], F32, name="sums")
+            z[b] = psum.tile([P, 1], F32, name="z")
             for t in range(TOKEN_BLOCKS):
+                products = work.tile([P, HEADS, PAIRS], F32, name="products")
                 for q in range(HEADS):
                     nc.vector.tensor_tensor(
-                        products[:, q, t], windows[b, q, t][:].indirect(picks), tails[b][:, q, t], MULT
+                        products[:, q], windows[b, q, t][:].indirect(picks), tails[b // 2, q][:, t, columns], MULT
                     )
-
-            weights = work.tile([P, TOKEN_BLOCKS, PAIRS], BF16, name="weights")
-            nc.vector.tensor_tensor(weights[:], products[:, 0], products[:, 1], ADD)
-
-            z_all = psum.tile([P, PAIRS], F32, name="z_all")
-            for t in range(TOKEN_BLOCKS):
-                nc.tensor.matmul(
-                    z_all[:], ones[:], weights[:, t], start=(t == 0), stop=(t == TOKEN_BLOCKS - 1)
-                )
-            z_inverse = work.tile([P, PAIRS], F32, name="z_inverse")
-            nc.vector.reciprocal(z_inverse[:], z_all[:])
-
-            pooled = work.tile([P, FEATURE_BLOCKS, PAIRS], F32, name="pooled")
-            for c in range(FEATURE_BLOCKS):
-                block = slice(c * P, (c + 1) * P)
-                sums = psum.tile([P, PAIRS], F32, name="sums")
-                for t in range(TOKEN_BLOCKS):
-                    nc.tensor.matmul(
-                        sums[:], features[b][:, t, block], weights[:, t],
-                        start=(t == 0), stop=(t == TOKEN_BLOCKS - 1),
-                    )
-                nc.vector.tensor_tensor(pooled[:, c], sums[:], z_inverse[:], MULT)
-            nc.sync.dma_start(out_rows[:, :, pairs], pooled[:])
+                weights = work.tile([P, PAIRS], BF16, name="weights")
+                nc.vector.tensor_tensor(weights[:], products[:, 0], products[:, 1], ADD)
+                first, last = t == 0, t == TOKEN_BLOCKS - 1
+                nc.tensor.matmul(sums[b][:], weights[:], features[b][:, t], start=first, stop=last)
+                nc.tensor.matmul(z[b][:], weights[:], ones[:], start=first, stop=last)
+                if first and b > 0:
+                    normalise_and_store(b - 1)
+        normalise_and_store(DOCS - 1)

@@ -47,12 +47,10 @@ def tile_my_model4_kernel(tc, x, t_att, context, offs, out):
         windows = {}
         tails = {}
         features = {}
+        for q in range(HEADS):
+            tails[q] = held.tile([P, TOKEN_BLOCKS, ENTRIES], F32, name=f"tail{q}")
+            queue[q].dma_start(tails[q][:], t_att_rows[q])
         for b in range(DOCS):
-            if b % 2 == 0:
-                columns = slice(b * PAIRS, (b + 2) * PAIRS)
-                for q in range(HEADS):
-                    tails[b // 2, q] = held.tile([P, TOKEN_BLOCKS, 2 * PAIRS], F32, name=f"tail{b // 2}{q}")
-                    queue[q].dma_start(tails[b // 2, q][:], t_att_rows[q, :, :, columns])
             for t in range(TOKEN_BLOCKS):
                 for q in range(HEADS):
                     windows[b, q, t] = held.tile([P, ENTITIES], F32, name=f"window{b}{q}{t}")
@@ -60,8 +58,30 @@ def tile_my_model4_kernel(tc, x, t_att, context, offs, out):
             features[b] = held.tile([P, TOKEN_BLOCKS, FEATURES], BF16, name=f"features{b}")
             queue[b % 2].dma_start(features[b][:], context_rows[b])
 
+        products = {}
         sums = {}
         z = {}
+
+        def multiply(b, t):
+            picks = offsets[:, b * (PAIRS // 16) : (b + 1) * (PAIRS // 16)]
+            products[b, t] = work.tile([P, HEADS, PAIRS], F32, name="products")
+            for q in range(HEADS):
+                nc.vector.tensor_tensor(
+                    products[b, t][:, q],
+                    windows[b, q, t][:].indirect(picks),
+                    tails[q][:, t, b * PAIRS : (b + 1) * PAIRS],
+                    MULT,
+                )
+
+        def add_and_pool(b, t):
+            weights = work.tile([P, PAIRS], BF16, name="weights")
+            nc.vector.tensor_tensor(weights[:], products[b, t][:, 0], products[b, t][:, 1], ADD)
+            first, last = t == 0, t == TOKEN_BLOCKS - 1
+            if first:
+                sums[b] = psum.tile([P, FEATURES], F32, name="sums")
+                z[b] = psum.tile([P, 1], F32, name="z")
+            nc.tensor.matmul(sums[b][:], weights[:], features[b][:, t], start=first, stop=last)
+            nc.tensor.matmul(z[b][:], weights[:], ones[:], start=first, stop=last)
 
         def normalise_and_store(b):
             z_inverse = work.tile([P, 1], F32, name="z_inverse")
@@ -75,22 +95,11 @@ def tile_my_model4_kernel(tc, x, t_att, context, offs, out):
             nc.scalar.copy(result[:], flipped[:])
             nc.sync.dma_start(out_rows[:, :, b * PAIRS : (b + 1) * PAIRS], result[:])
 
-        for b in range(DOCS):
-            picks = offsets[:, b * (PAIRS // 16) : (b + 1) * (PAIRS // 16)]
-            columns = slice((b % 2) * PAIRS, (b % 2 + 1) * PAIRS)
-            sums[b] = psum.tile([P, FEATURES], F32, name="sums")
-            z[b] = psum.tile([P, 1], F32, name="z")
-            for t in range(TOKEN_BLOCKS):
-                products = work.tile([P, HEADS, PAIRS], F32, name="products")
-                for q in range(HEADS):
-                    nc.vector.tensor_tensor(
-                        products[:, q], windows[b, q, t][:].indirect(picks), tails[b // 2, q][:, t, columns], MULT
-                    )
-                weights = work.tile([P, PAIRS], BF16, name="weights")
-                nc.vector.tensor_tensor(weights[:], products[:, 0], products[:, 1], ADD)
-                first, last = t == 0, t == TOKEN_BLOCKS - 1
-                nc.tensor.matmul(sums[b][:], weights[:], features[b][:, t], start=first, stop=last)
-                nc.tensor.matmul(z[b][:], weights[:], ones[:], start=first, stop=last)
-                if first and b > 0:
-                    normalise_and_store(b - 1)
-        normalise_and_store(DOCS - 1)
+        blocks = [(b, t) for b in range(DOCS) for t in range(TOKEN_BLOCKS)]
+        for step in range(len(blocks) + 2):
+            if step < len(blocks):
+                multiply(*blocks[step])
+            if 1 <= step <= len(blocks):
+                add_and_pool(*blocks[step - 1])
+            if step >= 2 and blocks[step - 2][1] == TOKEN_BLOCKS - 1:
+                normalise_and_store(blocks[step - 2][0])

@@ -6,7 +6,6 @@ BF16 = mybir.dt.bfloat16
 U16 = mybir.dt.uint16
 MULT = mybir.AluOpType.mult
 ADD = mybir.AluOpType.add
-COPY = mybir.ActivationFunctionType.Copy
 
 P = 128
 DOCS = 4
@@ -18,6 +17,8 @@ PAIRS = 128
 ENTRIES = DOCS * PAIRS
 TOKEN_BLOCKS = TOKENS // P
 FEATURE_BLOCKS = FEATURES // P
+HALVES = 2
+HALF = TOKEN_BLOCKS // HALVES
 
 FLOPS = 2 * TOKENS * (FEATURES + 1) * ENTRIES
 
@@ -26,7 +27,7 @@ def tile_my_model4_kernel(tc, x, t_att, context, offs, out):
     nc = tc.nc
 
     x_rows = x.rearrange("b (q p t) e -> b q t p e", q=HEADS, t=TOKEN_BLOCKS)
-    t_att_rows = t_att.rearrange("(q p t) j -> q p t j", q=HEADS, t=TOKEN_BLOCKS)
+    t_att_rows = t_att.rearrange("(q p h t) j -> q h p t j", q=HEADS, h=HALVES, t=HALF)
     context_rows = context.rearrange("b (p t) d -> b p t d", t=TOKEN_BLOCKS)
     out_rows = out.rearrange("(c p) j -> p c j", p=P)
 
@@ -34,6 +35,7 @@ def tile_my_model4_kernel(tc, x, t_att, context, offs, out):
         tc.tile_pool(name="held", bufs=1) as held,
         tc.tile_pool(name="work", bufs=4) as work,
         tc.psum_pool(name="psum", bufs=2) as psum,
+        tc.psum_pool(name="psum_held", bufs=1) as psum_held,
     ):
         offsets = held.tile([P, ENTRIES // 16], U16, name="offsets")
         nc.sync.dma_start(offsets[:], offs)
@@ -47,59 +49,95 @@ def tile_my_model4_kernel(tc, x, t_att, context, offs, out):
         windows = {}
         tails = {}
         features = {}
-        for q in range(HEADS):
-            tails[q] = held.tile([P, TOKEN_BLOCKS, ENTRIES], F32, name=f"tail{q}")
-            queue[q].dma_start(tails[q][:], t_att_rows[q])
-        for b in range(DOCS):
-            for t in range(TOKEN_BLOCKS):
-                for q in range(HEADS):
-                    windows[b, q, t] = held.tile([P, ENTITIES], F32, name=f"window{b}{q}{t}")
-                    queue[q].dma_start(windows[b, q, t][:], x_rows[b, q, t])
-            features[b] = held.tile([P, TOKEN_BLOCKS, FEATURES], BF16, name=f"features{b}")
-            queue[b % 2].dma_start(features[b][:], context_rows[b])
+        for h in range(HALVES):
+            for q in range(HEADS):
+                tails[q, h] = held.tile([P, HALF, ENTRIES], F32, name=f"tail{q}{h}")
+                queue[q].dma_start(tails[q, h][:], t_att_rows[q, h])
+            for b in range(DOCS):
+                for t in range(h * HALF, (h + 1) * HALF):
+                    for q in range(HEADS):
+                        windows[b, q, t] = held.tile([P, ENTITIES], F32, name=f"window{b}{q}{t}")
+                        queue[q].dma_start(windows[b, q, t][:], x_rows[b, q, t])
+                if h == HALVES - 1:
+                    features[b] = held.tile([P, TOKEN_BLOCKS, FEATURES], BF16, name=f"features{b}")
+                    queue[b % 2].dma_start(features[b][:], context_rows[b])
 
         products = {}
+        weights = {}
         sums = {}
         z = {}
+        z_inverse_rows = {}
 
-        def multiply(b, t):
+        def multiply(h, b, t):
             picks = offsets[:, b * (PAIRS // 16) : (b + 1) * (PAIRS // 16)]
-            products[b, t] = work.tile([P, HEADS, PAIRS], F32, name="products")
+            if t == 0:
+                products[h, b] = work.tile([P, HEADS, HALF, PAIRS], F32, name="products")
             for q in range(HEADS):
                 nc.vector.tensor_tensor(
-                    products[b, t][:, q],
-                    windows[b, q, t][:].indirect(picks),
-                    tails[q][:, t, b * PAIRS : (b + 1) * PAIRS],
+                    products[h, b][:, q, t],
+                    windows[b, q, h * HALF + t][:].indirect(picks),
+                    tails[q, h][:, t, b * PAIRS : (b + 1) * PAIRS],
                     MULT,
                 )
 
-        def add_and_pool(b, t):
-            weights = work.tile([P, PAIRS], BF16, name="weights")
-            nc.vector.tensor_tensor(weights[:], products[b, t][:, 0], products[b, t][:, 1], ADD)
-            first, last = t == 0, t == TOKEN_BLOCKS - 1
-            if first:
-                sums[b] = psum.tile([P, FEATURES], F32, name="sums")
-                z[b] = psum.tile([P, 1], F32, name="z")
-            nc.tensor.matmul(sums[b][:], weights[:], features[b][:, t], start=first, stop=last)
-            nc.tensor.matmul(z[b][:], weights[:], ones[:], start=first, stop=last)
+        def add_heads(h, b):
+            weights[h, b] = held.tile([P, HALF, PAIRS], BF16, name=f"weights{h}{b}")
+            nc.vector.tensor_tensor(weights[h, b][:], products[h, b][:, 0], products[h, b][:, 1], ADD)
 
-        def normalise_and_store(b):
+        def total(b):
+            z[b] = psum.tile([P, 1], F32, name="z")
+            for t in range(TOKEN_BLOCKS):
+                nc.tensor.matmul(
+                    z[b][:], weights[t // HALF, b][:, t % HALF], ones[:], start=t == 0, stop=t == TOKEN_BLOCKS - 1
+                )
+
+        def pool(b, c):
+            if c == 0:
+                sums[b] = psum_held.tile([P, FEATURE_BLOCKS, PAIRS], F32, name=f"sums{b}")
+            for t in range(TOKEN_BLOCKS):
+                nc.tensor.matmul(
+                    sums[b][:, c],
+                    features[b][:, t, c * P : (c + 1) * P],
+                    weights[t // HALF, b][:, t % HALF],
+                    start=t == 0,
+                    stop=t == TOKEN_BLOCKS - 1,
+                )
+
+        def invert(b):
             z_inverse = work.tile([P, 1], F32, name="z_inverse")
             nc.vector.reciprocal(z_inverse[:], z[b][:])
-            pooled = work.tile([P, FEATURES], F32, name="pooled")
-            nc.scalar.activation(pooled[:], sums[b][:], COPY, scale=z_inverse[:])
-            flipped = psum.tile([P, FEATURE_BLOCKS, PAIRS], F32, name="flipped")
-            for c in range(FEATURE_BLOCKS):
-                nc.tensor.transpose(flipped[:, c], pooled[:, c * P : (c + 1) * P], identity[:])
+            spread = psum.tile([P, PAIRS], F32, name="spread")
+            nc.tensor.matmul(spread[:], z_inverse[:].to_broadcast([P, P]), identity[:], start=True, stop=True)
+            z_inverse_rows[b] = held.tile([P, PAIRS], F32, name=f"z_inverse_rows{b}")
+            nc.scalar.copy(z_inverse_rows[b][:], spread[:])
+
+        def finish(b):
             result = work.tile([P, FEATURE_BLOCKS, PAIRS], F32, name="result")
-            nc.scalar.copy(result[:], flipped[:])
+            for c in range(FEATURE_BLOCKS):
+                nc.vector.tensor_tensor(result[:, c], sums[b][:, c], z_inverse_rows[b][:], MULT)
             nc.sync.dma_start(out_rows[:, :, b * PAIRS : (b + 1) * PAIRS], result[:])
 
-        blocks = [(b, t) for b in range(DOCS) for t in range(TOKEN_BLOCKS)]
-        for step in range(len(blocks) + 2):
-            if step < len(blocks):
-                multiply(*blocks[step])
-            if 1 <= step <= len(blocks):
-                add_and_pool(*blocks[step - 1])
-            if step >= 2 and blocks[step - 2][1] == TOKEN_BLOCKS - 1:
-                normalise_and_store(blocks[step - 2][0])
+        FINISH_LAG = 3
+        units = [(h, b) for h in range(HALVES) for b in range(DOCS)]
+
+        def completed(step):
+            if 0 <= step < len(units) and units[step][0] == HALVES - 1:
+                return units[step][1]
+            return None
+
+        for step in range(len(units) + FINISH_LAG):
+            done = completed(step - 1)
+            if step < len(units):
+                multiply(*units[step], 0)
+            if 1 <= step <= len(units):
+                add_heads(*units[step - 1])
+            if done is not None:
+                total(done)
+                pool(done, 0)
+            if step < len(units):
+                multiply(*units[step], 1)
+            if done is not None:
+                invert(done)
+                pool(done, 1)
+            if completed(step - FINISH_LAG) is not None:
+                finish(completed(step - FINISH_LAG))

@@ -35,7 +35,7 @@ def tile_my_model4_kernel(tc, x, t_att, context, offs, out):
         tc.tile_pool(name="held", bufs=1) as held,
         tc.tile_pool(name="work", bufs=4) as work,
         tc.psum_pool(name="psum", bufs=2) as psum,
-        tc.psum_pool(name="psum_held", bufs=1) as psum_held,
+        tc.psum_pool(name="psum_sums", bufs=2 * FEATURE_BLOCKS) as psum_sums,
     ):
         offsets = held.tile([P, ENTRIES // 16], U16, name="offsets")
         nc.sync.dma_start(offsets[:], offs)
@@ -84,21 +84,22 @@ def tile_my_model4_kernel(tc, x, t_att, context, offs, out):
             weights[h, b] = held.tile([P, HALF, PAIRS], BF16, name=f"weights{h}{b}")
             nc.vector.tensor_tensor(weights[h, b][:], products[h, b][:, 0], products[h, b][:, 1], ADD)
 
-        def total(b):
-            z[b] = psum.tile([P, 1], F32, name="z")
-            for t in range(TOKEN_BLOCKS):
+        def total(b, h):
+            if h == 0:
+                z[b] = psum.tile([P, 1], F32, name="z")
+            for t in range(h * HALF, (h + 1) * HALF):
                 nc.tensor.matmul(
-                    z[b][:], weights[t // HALF, b][:, t % HALF], ones[:], start=t == 0, stop=t == TOKEN_BLOCKS - 1
+                    z[b][:], weights[h, b][:, t % HALF], ones[:], start=t == 0, stop=t == TOKEN_BLOCKS - 1
                 )
 
-        def pool(b, c):
-            if c == 0:
-                sums[b] = psum_held.tile([P, FEATURE_BLOCKS, PAIRS], F32, name=f"sums{b}")
-            for t in range(TOKEN_BLOCKS):
+        def pool(b, c, h):
+            if h == 0:
+                sums[b, c] = psum_sums.tile([P, PAIRS], F32, name="sums")
+            for t in range(h * HALF, (h + 1) * HALF):
                 nc.tensor.matmul(
-                    sums[b][:, c],
+                    sums[b, c][:],
                     features[b][:, t, c * P : (c + 1) * P],
-                    weights[t // HALF, b][:, t % HALF],
+                    weights[h, b][:, t % HALF],
                     start=t == 0,
                     stop=t == TOKEN_BLOCKS - 1,
                 )
@@ -114,10 +115,10 @@ def tile_my_model4_kernel(tc, x, t_att, context, offs, out):
         def finish(b):
             result = work.tile([P, FEATURE_BLOCKS, PAIRS], F32, name="result")
             for c in range(FEATURE_BLOCKS):
-                nc.vector.tensor_tensor(result[:, c], sums[b][:, c], z_inverse_rows[b][:], MULT)
+                nc.vector.tensor_tensor(result[:, c], sums[b, c][:], z_inverse_rows[b][:], MULT)
             nc.sync.dma_start(out_rows[:, :, b * PAIRS : (b + 1) * PAIRS], result[:])
 
-        FINISH_LAG = 3
+        FINISH_LAG = 2
         units = [(h, b) for h in range(HALVES) for b in range(DOCS)]
 
         def completed(step):
@@ -132,12 +133,16 @@ def tile_my_model4_kernel(tc, x, t_att, context, offs, out):
             if 1 <= step <= len(units):
                 add_heads(*units[step - 1])
             if done is not None:
-                total(done)
-                pool(done, 0)
+                total(done, 1)
+                for c in range(FEATURE_BLOCKS):
+                    pool(done, c, 1)
             if step < len(units):
                 multiply(*units[step], 1)
             if done is not None:
                 invert(done)
-                pool(done, 1)
             if completed(step - FINISH_LAG) is not None:
                 finish(completed(step - FINISH_LAG))
+            if completed(step) is not None:
+                total(completed(step), 0)
+                for c in range(FEATURE_BLOCKS):
+                    pool(completed(step), c, 0)

@@ -108,7 +108,7 @@ def tile_my_model4_kernel(tc, x, t_att, context, offs, out):
             z_inverse = work.tile([P, 1], F32, name="z_inverse")
             nc.vector.reciprocal(z_inverse[:], z[b][:])
             spread = psum.tile([P, PAIRS], F32, name="spread")
-            nc.tensor.matmul(spread[:], z_inverse[:].to_broadcast([P, P]), identity[:], start=True, stop=True)
+            nc.tensor.transpose(spread[:], z_inverse[:].to_broadcast([P, P]), identity[:])
             z_inverse_rows[b] = held.tile([P, PAIRS], F32, name=f"z_inverse_rows{b}")
             nc.scalar.copy(z_inverse_rows[b][:], spread[:])
 

@@ -44,6 +44,8 @@ def tile_my_model4_kernel(tc, x, t_att, context, offs, out):
         nc.vector.memset(ones[:], 1.0)
         identity = held.tile([P, P], F32, name="identity")
         make_identity(nc, identity[:])
+        table_warmer = held.tile([P, 1], BF16, name="table_warmer")
+        nc.scalar.copy(table_warmer[:], ones[:])
 
         queue = (nc.sync, nc.scalar)
         windows = {}

@@ -35,7 +35,7 @@ def tile_my_model4_kernel(tc, x, t_att, context, offs, out):
         tc.tile_pool(name="held", bufs=1) as held,
         tc.tile_pool(name="work", bufs=4) as work,
         tc.psum_pool(name="psum", bufs=2) as psum,
-        tc.psum_pool(name="psum_sums", bufs=2 * FEATURE_BLOCKS) as psum_sums,
+        tc.psum_pool(name="psum_sums", bufs=3 * FEATURE_BLOCKS) as psum_sums,
     ):
         offsets = held.tile([P, ENTRIES // 16], U16, name="offsets")
         nc.sync.dma_start(offsets[:], offs)
@@ -68,6 +68,7 @@ def tile_my_model4_kernel(tc, x, t_att, context, offs, out):
         weights = {}
         sums = {}
         z = {}
+        spread = {}
         z_inverse_rows = {}
 
         def multiply(h, b, t):
@@ -88,10 +89,12 @@ def tile_my_model4_kernel(tc, x, t_att, context, offs, out):
 
         def total(b, h):
             if h == 0:
-                z[b] = psum.tile([P, 1], F32, name="z")
+                scale_bank = psum.tile([P, PAIRS + 1], F32, name="scale_bank")
+                spread[b] = scale_bank[:, :PAIRS]
+                z[b] = scale_bank[:, PAIRS:]
             for t in range(h * HALF, (h + 1) * HALF):
                 nc.tensor.matmul(
-                    z[b][:], weights[h, b][:, t % HALF], ones[:], start=t == 0, stop=t == TOKEN_BLOCKS - 1
+                    z[b], weights[h, b][:, t % HALF], ones[:], start=t == 0, stop=t == TOKEN_BLOCKS - 1
                 )
 
         def pool(b, c, h):
@@ -108,11 +111,10 @@ def tile_my_model4_kernel(tc, x, t_att, context, offs, out):
 
         def invert(b):
             z_inverse = work.tile([P, 1], F32, name="z_inverse")
-            nc.vector.reciprocal(z_inverse[:], z[b][:])
-            spread = psum.tile([P, PAIRS], F32, name="spread")
-            nc.tensor.transpose(spread[:], z_inverse[:].to_broadcast([P, P]), identity[:])
+            nc.vector.reciprocal(z_inverse[:], z[b])
+            nc.tensor.transpose(spread[b], z_inverse[:].to_broadcast([P, P]), identity[:])
             z_inverse_rows[b] = held.tile([P, PAIRS], F32, name=f"z_inverse_rows{b}")
-            nc.scalar.copy(z_inverse_rows[b][:], spread[:])
+            nc.scalar.copy(z_inverse_rows[b][:], spread[b])
 
         def finish(b):
             result = work.tile([P, FEATURE_BLOCKS, PAIRS], F32, name="result")
@@ -120,7 +122,7 @@ def tile_my_model4_kernel(tc, x, t_att, context, offs, out):
                 nc.vector.tensor_tensor(result[:, c], sums[b, c][:], z_inverse_rows[b][:], MULT)
             nc.sync.dma_start(out_rows[:, :, b * PAIRS : (b + 1) * PAIRS], result[:])
 
-        FINISH_LAG = 2
+        FINISH_LAG = 3
         units = [(h, b) for h in range(HALVES) for b in range(DOCS)]
 
         def completed(step):

import concourse.mybir as mybir
from concourse.masks import make_identity

F32 = mybir.dt.float32
BF16 = mybir.dt.bfloat16
U16 = mybir.dt.uint16
MULT = mybir.AluOpType.mult
ADD = mybir.AluOpType.add

P = 128
DOCS = 4
HEADS = 2
TOKENS = 512
ENTITIES = 256
FEATURES = 256
PAIRS = 128
ENTRIES = DOCS * PAIRS
TOKEN_BLOCKS = TOKENS // P
FEATURE_BLOCKS = FEATURES // P
HALVES = 2
HALF = TOKEN_BLOCKS // HALVES

FLOPS = 2 * TOKENS * (FEATURES + 1) * ENTRIES


def tile_my_model4_kernel(tc, x, t_att, context, offs, out):
    nc = tc.nc

    x_rows = x.rearrange("b (q p t) e -> b q t p e", q=HEADS, t=TOKEN_BLOCKS)
    t_att_rows = t_att.rearrange("(q p h t) j -> q h p t j", q=HEADS, h=HALVES, t=HALF)
    context_rows = context.rearrange("b (p t) d -> b p t d", t=TOKEN_BLOCKS)
    out_rows = out.rearrange("(c p) j -> p c j", p=P)

    with (
        tc.tile_pool(name="held", bufs=1) as held,
        tc.tile_pool(name="work", bufs=4) as work,
        tc.psum_pool(name="psum", bufs=2) as psum,
        tc.psum_pool(name="psum_sums", bufs=3 * FEATURE_BLOCKS) as psum_sums,
    ):
        offsets = held.tile([P, ENTRIES // 16], U16, name="offsets")
        nc.sync.dma_start(offsets[:], offs)

        ones = held.tile([P, 1], BF16, name="ones")
        nc.vector.memset(ones[:], 1.0)
        identity = held.tile([P, P], F32, name="identity")
        make_identity(nc, identity[:])
        table_warmer = held.tile([P, 1], BF16, name="table_warmer")
        nc.scalar.copy(table_warmer[:], ones[:])

        queue = (nc.sync, nc.scalar)
        windows = {}
        tails = {}
        features = {}
        for h in range(HALVES):
            for q in range(HEADS):
                tails[q, h] = held.tile([P, HALF, ENTRIES], F32, name=f"tail{q}{h}")
                queue[q].dma_start(tails[q, h][:], t_att_rows[q, h])
            for b in range(DOCS):
                for t in range(h * HALF, (h + 1) * HALF):
                    for q in range(HEADS):
                        windows[b, q, t] = held.tile([P, ENTITIES], F32, name=f"window{b}{q}{t}")
                        queue[q].dma_start(windows[b, q, t][:], x_rows[b, q, t])
                if h == HALVES - 1:
                    features[b] = held.tile([P, TOKEN_BLOCKS, FEATURES], BF16, name=f"features{b}")
                    queue[b % 2].dma_start(features[b][:], context_rows[b])

        products = {}
        weights = {}
        sums = {}
        z = {}
        spread = {}
        z_inverse_rows = {}

        def multiply(h, b, t):
            picks = offsets[:, b * (PAIRS // 16) : (b + 1) * (PAIRS // 16)]
            if t == 0:
                products[h, b] = work.tile([P, HEADS, HALF, PAIRS], F32, name="products")
            for q in range(HEADS):
                nc.vector.tensor_tensor(
                    products[h, b][:, q, t],
                    windows[b, q, h * HALF + t][:].indirect(picks),
                    tails[q, h][:, t, b * PAIRS : (b + 1) * PAIRS],
                    MULT,
                )

        def add_heads(h, b):
            weights[h, b] = held.tile([P, HALF, PAIRS], BF16, name=f"weights{h}{b}")
            nc.vector.tensor_tensor(weights[h, b][:], products[h, b][:, 0], products[h, b][:, 1], ADD)

        def total(b, h):
            if h == 0:
                scale_bank = psum.tile([P, PAIRS + 1], F32, name="scale_bank")
                spread[b] = scale_bank[:, :PAIRS]
                z[b] = scale_bank[:, PAIRS:]
            for t in range(h * HALF, (h + 1) * HALF):
                nc.tensor.matmul(
                    z[b], weights[h, b][:, t % HALF], ones[:], start=t == 0, stop=t == TOKEN_BLOCKS - 1
                )

        def pool(b, c, h):
            if h == 0:
                sums[b, c] = psum_sums.tile([P, PAIRS], F32, name="sums")
            for t in range(h * HALF, (h + 1) * HALF):
                nc.tensor.matmul(
                    sums[b, c][:],
                    features[b][:, t, c * P : (c + 1) * P],
                    weights[h, b][:, t % HALF],
                    start=t == 0,
                    stop=t == TOKEN_BLOCKS - 1,
                )

        def invert(b):
            z_inverse = work.tile([P, 1], F32, name="z_inverse")
            nc.vector.reciprocal(z_inverse[:], z[b])
            nc.tensor.transpose(spread[b], z_inverse[:].to_broadcast([P, P]), identity[:])
            z_inverse_rows[b] = held.tile([P, PAIRS], F32, name=f"z_inverse_rows{b}")
            nc.scalar.copy(z_inverse_rows[b][:], spread[b])

        def finish(b):
            result = work.tile([P, FEATURE_BLOCKS, PAIRS], F32, name="result")
            for c in range(FEATURE_BLOCKS):
                nc.vector.tensor_tensor(result[:, c], sums[b, c][:], z_inverse_rows[b][:], MULT)
            nc.sync.dma_start(out_rows[:, :, b * PAIRS : (b + 1) * PAIRS], result[:])

        FINISH_LAG = 3
        units = [(h, b) for h in range(HALVES) for b in range(DOCS)]

        def completed(step):
            if 0 <= step < len(units) and units[step][0] == HALVES - 1:
                return units[step][1]
            return None

        for step in range(len(units) + FINISH_LAG):
            done = completed(step - 1)
            if step < len(units):
                multiply(*units[step], 0)
            if 1 <= step <= len(units):
                add_heads(*units[step - 1])
            if done is not None:
                total(done, 1)
                for c in range(FEATURE_BLOCKS):
                    pool(done, c, 1)
            if step < len(units):
                multiply(*units[step], 1)
            if done is not None:
                invert(done)
            if completed(step - FINISH_LAG) is not None:
                finish(completed(step - FINISH_LAG))
            if completed(step) is not None:
                total(completed(step), 0)
                for c in range(FEATURE_BLOCKS):
                    pool(completed(step), c, 0)
